import numpy as np
import ml_dtypes


def mxq(x, axis, fmt="e4m3"):
    dtype, down = {"e4m3": (ml_dtypes.float8_e4m3fn, 7), "e5m2": (ml_dtypes.float8_e5m2, 14)}[fmt]
    v = np.moveaxis(np.asarray(x, np.float32).astype(ml_dtypes.bfloat16).astype(np.float64), axis, -1)
    blocks = v.reshape(v.shape[:-1] + (-1, 32))
    amax = np.abs(blocks).max(-1, keepdims=True)
    byte = np.maximum(np.where(amax > 0, np.frexp(amax)[1] - 1 + 127, 0) - down, 1)
    scale = np.exp2(byte - 127.0)
    codes = (blocks / scale).astype(np.float32).astype(dtype).astype(np.float64)
    return np.moveaxis((codes * scale).reshape(v.shape), -1, axis)


WIDE = False


def mx_kscale(k):
    if not WIDE:
        return np.ones(k)
    levels = np.array([10, -10, 5, -5, 0])
    a = np.random.permutation(np.resize(levels, k // 512 * 4)).reshape(k // 512, 4)
    idx = np.arange(k)
    return np.exp2(a[idx // 512, idx % 128 // 32])


BF16 = ml_dtypes.bfloat16


def bf(x):
    return np.asarray(x, np.float32).astype(BF16)


def f64(x):
    return np.asarray(x).astype(np.float64)


IN, H, C, B = 8192, 512, 2, 128
QH = H % 512 == 0


def sigmoid(v):
    return 1.0 / (1.0 + np.exp(-v))


def setup_inputs():
    s = mx_kscale(IN)
    t = mx_kscale(H) if QH else np.ones(H)
    return {"input_word": bf(np.random.standard_normal((B, IN)) * s),
            "hidden_states": bf(np.random.standard_normal((B, H)) * t),
            "Wx": bf(np.random.uniform(-1.0, 1.0, (C, 2 * H, IN)) / np.sqrt(IN) / s),
            "bx": bf(np.random.standard_normal((C, 2 * H)) * 0.3),
            "Wh": bf(np.random.uniform(-1.0, 1.0, (C, 2 * H, H)) / np.sqrt(H) / t)}


def reference(input_word, hidden_states, Wx, bx, Wh):
    px = mxq(f64(input_word), 1, "e4m3") @ mxq(f64(Wx), 2, "e4m3").transpose(0, 2, 1)
    if QH:
        ph = mxq(f64(hidden_states), 1, "e4m3") @ mxq(f64(Wh), 2, "e4m3").transpose(0, 2, 1)
    else:
        ph = f64(hidden_states) @ f64(Wh).transpose(0, 2, 1)
    net = px.transpose(1, 0, 2) + ph.transpose(1, 0, 2) + f64(bx)[None, :, :]
    input_gate, cell_states = net[..., :H], net[..., H:]
    cell_input = np.tanh(cell_states)
    input_gate = sigmoid(input_gate)
    return (cell_input, input_gate)

@@ -1,0 +1,204 @@
+from contextlib import ExitStack
+
+import concourse.masks as masks
+import concourse.mybir as mybir
+
+F32 = mybir.dt.float32
+BF16 = mybir.dt.bfloat16
+I32 = mybir.dt.int32
+U32 = mybir.dt.uint32
+U8 = mybir.dt.uint8
+FP8X4 = mybir.dt.float8_e4m3fn_x4
+ACT = mybir.ActivationFunctionType
+ALU = mybir.AluOpType
+
+P = 128
+PACK = 4
+K_PASS = P * PACK
+IN = 8192
+H = 512
+CELLS = 2
+X_PASSES = IN // K_PASS
+BLOCKS = CELLS * 2 * H // P
+BLOCKS_PER_GATE = H // P
+
+WORDS_PER_PASS = K_PASS // 2
+BANK_WORDS = 512
+PASSES_PER_BANK = BANK_WORDS // WORDS_PER_PASS
+UNIT_BANKS = X_PASSES // PASSES_PER_BANK
+
+QUANTISE_LAG = 2
+VECTOR_COPY_EVERY = 4
+
+RAW_BUFS = 6
+TRANSPOSE_BANKS = 6
+SUM_BANKS = 2
+
+FLOPS = 2 * P * (CELLS * 2 * H) * (IN + H)
+
+
+def tile_compute_gate_k_kernel(tc, input_word, hidden_states, Wx, bx, Wh, out_0, out_1):
+    nc = tc.nc
+    with ExitStack() as ctx:
+        keep = ctx.enter_context(tc.tile_pool(name="keep", bufs=1))
+        raw_pool = ctx.enter_context(tc.tile_pool(name="raw", bufs=RAW_BUFS))
+        grouped_pool = ctx.enter_context(tc.tile_pool(name="grouped", bufs=QUANTISE_LAG + 3))
+        weight_pool = ctx.enter_context(tc.tile_pool(name="weight", bufs=3))
+        out_pool = ctx.enter_context(tc.tile_pool(name="out", bufs=2))
+        banks = ctx.enter_context(tc.psum_pool(name="banks", bufs=TRANSPOSE_BANKS))
+        sums = ctx.enter_context(tc.psum_pool(name="sums", bufs=SUM_BANKS))
+        ctx.enter_context(tc.manual_schedule())
+
+        def load_unit(rows):
+            raw = raw_pool.tile([P, IN], BF16, name="raw")
+            if rows.ndim == 2:
+                nc.sync.dma_start(out=raw[:], in_=rows)
+            else:
+                nc.sync.dma_start(out=raw[:].rearrange("p (b k) -> p b k", k=H), in_=rows)
+            return raw
+
+        def transpose_bank(words, passes, on_vector):
+            bank = banks.tile([P, BANK_WORDS], F32, name="bank")
+            for i in range(2 * passes):
+                cols = slice(i * P, (i + 1) * P)
+                nc.tensor.transpose(bank[:, cols], words[:, cols], identity[:])
+            grouped = grouped_pool.tile([P, passes * P * PACK], BF16, name="grouped", align_bytes=64)
+            regrouped = bank[:, : 2 * passes * P].rearrange("p (g u r) -> p g r u", u=2, r=P)
+            target = grouped[:].bitcast(F32).rearrange("p (g r u) -> p g r u", u=2, r=P)
+            if on_vector:
+                nc.vector.tensor_copy(out=target, in_=regrouped)
+            else:
+                nc.scalar.copy(out=target, in_=regrouped)
+            return grouped
+
+        def transpose_and_quantise(raw, codes, scales):
+            words = raw[:].bitcast(F32)
+            grouped_tiles = []
+            for b in range(UNIT_BANKS + QUANTISE_LAG):
+                if b < UNIT_BANKS:
+                    bank_words = words[:, b * BANK_WORDS : (b + 1) * BANK_WORDS]
+                    on_vector = b % VECTOR_COPY_EVERY == VECTOR_COPY_EVERY - 1
+                    grouped_tiles.append(transpose_bank(bank_words, PASSES_PER_BANK, on_vector))
+                if b >= QUANTISE_LAG:
+                    ready = b - QUANTISE_LAG
+                    cols = slice(ready * PASSES_PER_BANK * P, (ready + 1) * PASSES_PER_BANK * P)
+                    nc.vector.quantize_mx(
+                        out=codes[:, cols].bitcast(FP8X4),
+                        scales=scales[:, cols],
+                        in_=grouped_tiles[ready][:],
+                    )
+
+        block_order = []
+        for gate in range(2):
+            for cell in range(CELLS):
+                for quarter in range(BLOCKS_PER_GATE):
+                    block_order.append((gate, cell, quarter))
+
+        def wx_rows(i):
+            gate, cell, quarter = block_order[i]
+            first = (gate * BLOCKS_PER_GATE + quarter) * P
+            return Wx[cell, first : first + P, :]
+
+        x_raw = load_unit(input_word)
+        h_raw = keep.tile([P, H], BF16, name="h_raw")
+        nc.sync.dma_start(out=h_raw[:], in_=hidden_states)
+        bias_rows = keep.tile([P, CELLS * 2 * H], BF16, name="bias_rows")
+        nc.vector.memset(bias_rows[:].bitcast(I32), 0)
+        nc.sync.dma_start(out=bias_rows[0:1, :], in_=bx.rearrange("(o c) n -> o (c n)", o=1))
+        wh_raw = load_unit(Wh.rearrange("c (b p) k -> p (c b) k", p=P))
+        wx_raw = [load_unit(wx_rows(i)) for i in range(RAW_BUFS - 2)]
+
+        identity = keep.tile([P, P], F32, name="identity")
+        masks.make_identity(nc, identity[:])
+        ones = keep.tile([P, P], BF16, name="ones")
+        nc.vector.memset(ones[:], 1.0)
+
+        x_codes = keep.tile([P, X_PASSES * P], U32, name="x_codes", align_bytes=64)
+        x_scales = keep.tile([P, X_PASSES * P], U8, name="x_scales", align_bytes=64)
+        transpose_and_quantise(x_raw, x_codes, x_scales)
+        wx_raw.append(load_unit(wx_rows(len(wx_raw))))
+
+        h_codes = keep.tile([P, P], U32, name="h_codes", align_bytes=64)
+        h_scales = keep.tile([P, P], U8, name="h_scales", align_bytes=64)
+        h_grouped = transpose_bank(h_raw[:].bitcast(F32), 1, False)
+
+        bias = keep.tile([P, CELLS * 2 * H], F32, name="bias")
+        for j in range(CELLS * 2 * H // BANK_WORDS):
+            cols = slice(j * BANK_WORDS, (j + 1) * BANK_WORDS)
+            spread = banks.tile([P, BANK_WORDS], F32, name="bank")
+            nc.tensor.matmul(out=spread[:], lhsT=ones[:], rhs=bias_rows[:, cols], start=True, stop=True)
+            nc.vector.tensor_copy(out=bias[:, cols], in_=spread[:])
+        nc.vector.quantize_mx(out=h_codes[:].bitcast(FP8X4), scales=h_scales[:], in_=h_grouped[:])
+
+        wh_codes = keep.tile([P, BLOCKS * P], U32, name="wh_codes", align_bytes=64)
+        wh_scales = keep.tile([P, BLOCKS * P], U8, name="wh_scales", align_bytes=64)
+        transpose_and_quantise(wh_raw, wh_codes, wh_scales)
+        wx_raw.append(load_unit(wx_rows(len(wx_raw))))
+
+        wx_codes = []
+        wx_scales = []
+        net_sums = []
+        results = []
+
+        def prepare(i):
+            codes = weight_pool.tile([P, X_PASSES * P], U32, name="codes", align_bytes=64)
+            scales = weight_pool.tile([P, X_PASSES * P], U8, name="scales", align_bytes=64)
+            transpose_and_quantise(wx_raw[i], codes, scales)
+            wx_codes.append(codes)
+            wx_scales.append(scales)
+            if len(wx_raw) < BLOCKS:
+                wx_raw.append(load_unit(wx_rows(len(wx_raw))))
+
+        def multiply(i):
+            gate, cell, quarter = block_order[i]
+            acc = sums.tile([P, P], F32, name="acc")
+            for g in range(X_PASSES):
+                cols = slice(g * P, (g + 1) * P)
+                nc.tensor.matmul_mx(
+                    out=acc[:],
+                    lhsT=x_codes[:, cols].bitcast(FP8X4),
+                    lhsT_scale=x_scales[:, cols],
+                    rhs=wx_codes[i][:, cols].bitcast(FP8X4),
+                    rhs_scale=wx_scales[i][:, cols],
+                    start=(g == 0),
+                    stop=False,
+                )
+            block = cell * 2 * BLOCKS_PER_GATE + gate * BLOCKS_PER_GATE + quarter
+            cols = slice(block * P, (block + 1) * P)
+            nc.tensor.matmul_mx(
+                out=acc[:],
+                lhsT=h_codes[:].bitcast(FP8X4),
+                lhsT_scale=h_scales[:],
+                rhs=wh_codes[:, cols].bitcast(FP8X4),
+                rhs_scale=wh_scales[:, cols],
+                start=False,
+                stop=True,
+            )
+            net_sums.append(acc)
+
+        def finish(i):
+            gate, cell, quarter = block_order[i]
+            block = cell * 2 * BLOCKS_PER_GATE + gate * BLOCKS_PER_GATE + quarter
+            if quarter == 0:
+                results.append(out_pool.tile([P, H], F32, name="result"))
+            result = results[-1]
+            net = out_pool.tile([P, P], F32, name="net")
+            nc.vector.tensor_tensor(
+                out=net[:], in0=net_sums[i][:], in1=bias[:, block * P : (block + 1) * P], op=ALU.add
+            )
+            nc.scalar.activation(
+                out=result[:, quarter * P : (quarter + 1) * P],
+                in_=net[:],
+                func=ACT.Sigmoid if gate == 0 else ACT.Tanh,
+            )
+            if quarter == BLOCKS_PER_GATE - 1:
+                out = out_1 if gate == 0 else out_0
+                nc.sync.dma_start(out=out[:, cell, :], in_=result[:])
+
+        for i in range(BLOCKS + 2):
+            if i < BLOCKS:
+                prepare(i)
+            if 1 <= i <= BLOCKS:
+                multiply(i - 1)
+            if i >= 2:
+                finish(i - 2)

@@ -26,9 +26,15 @@ WORDS_PER_PASS = K_PASS // 2
 BANK_WORDS = 512
 PASSES_PER_BANK = BANK_WORDS // WORDS_PER_PASS
 UNIT_BANKS = X_PASSES // PASSES_PER_BANK
+RUN_BANKS = 4
+UNIT_RUNS = UNIT_BANKS // RUN_BANKS
+RUN_PASSES = RUN_BANKS * PASSES_PER_BANK
 
 QUANTISE_LAG = 2
 VECTOR_COPY_EVERY = 4
+
+MULTIPLY_LAG = 2
+FINISH_LAG = 1
 
 RAW_BUFS = 6
 TRANSPOSE_BANKS = 6
@@ -71,17 +77,20 @@ def tile_compute_gate_k_kernel(tc, input_word, hidden_states, Wx, bx, Wh, out_0,
                 nc.scalar.copy(out=target, in_=regrouped)
             return grouped
 
-        def transpose_and_quantise(raw, codes, scales):
+        def transpose_and_quantise(raw, codes, scales, run):
             words = raw[:].bitcast(F32)
             grouped_tiles = []
-            for b in range(UNIT_BANKS + QUANTISE_LAG):
-                if b < UNIT_BANKS:
-                    bank_words = words[:, b * BANK_WORDS : (b + 1) * BANK_WORDS]
+            for b in range(RUN_BANKS + QUANTISE_LAG):
+                if b < RUN_BANKS:
+                    first = (run * RUN_BANKS + b) * BANK_WORDS
                     on_vector = b % VECTOR_COPY_EVERY == VECTOR_COPY_EVERY - 1
-                    grouped_tiles.append(transpose_bank(bank_words, PASSES_PER_BANK, on_vector))
+                    grouped_tiles.append(
+                        transpose_bank(words[:, first : first + BANK_WORDS], PASSES_PER_BANK, on_vector)
+                    )
                 if b >= QUANTISE_LAG:
                     ready = b - QUANTISE_LAG
-                    cols = slice(ready * PASSES_PER_BANK * P, (ready + 1) * PASSES_PER_BANK * P)
+                    first = (run * RUN_BANKS + ready) * PASSES_PER_BANK * P
+                    cols = slice(first, first + PASSES_PER_BANK * P)
                     nc.vector.quantize_mx(
                         out=codes[:, cols].bitcast(FP8X4),
                         scales=scales[:, cols],
@@ -115,7 +124,8 @@ def tile_compute_gate_k_kernel(tc, input_word, hidden_states, Wx, bx, Wh, out_0,
 
         x_codes = keep.tile([P, X_PASSES * P], U32, name="x_codes", align_bytes=64)
         x_scales = keep.tile([P, X_PASSES * P], U8, name="x_scales", align_bytes=64)
-        transpose_and_quantise(x_raw, x_codes, x_scales)
+        for run in range(UNIT_RUNS):
+            transpose_and_quantise(x_raw, x_codes, x_scales, run)
         wx_raw.append(load_unit(wx_rows(len(wx_raw))))
 
         h_codes = keep.tile([P, P], U32, name="h_codes", align_bytes=64)
@@ -132,7 +142,8 @@ def tile_compute_gate_k_kernel(tc, input_word, hidden_states, Wx, bx, Wh, out_0,
 
         wh_codes = keep.tile([P, BLOCKS * P], U32, name="wh_codes", align_bytes=64)
         wh_scales = keep.tile([P, BLOCKS * P], U8, name="wh_scales", align_bytes=64)
-        transpose_and_quantise(wh_raw, wh_codes, wh_scales)
+        for run in range(UNIT_RUNS):
+            transpose_and_quantise(wh_raw, wh_codes, wh_scales, run)
         wx_raw.append(load_unit(wx_rows(len(wx_raw))))
 
         wx_codes = []
@@ -140,19 +151,20 @@ def tile_compute_gate_k_kernel(tc, input_word, hidden_states, Wx, bx, Wh, out_0,
         net_sums = []
         results = []
 
-        def prepare(i):
-            codes = weight_pool.tile([P, X_PASSES * P], U32, name="codes", align_bytes=64)
-            scales = weight_pool.tile([P, X_PASSES * P], U8, name="scales", align_bytes=64)
-            transpose_and_quantise(wx_raw[i], codes, scales)
-            wx_codes.append(codes)
-            wx_scales.append(scales)
-            if len(wx_raw) < BLOCKS:
+        def prepare(i, run):
+            if run == 0:
+                wx_codes.append(weight_pool.tile([P, X_PASSES * P], U32, name="codes", align_bytes=64))
+                wx_scales.append(weight_pool.tile([P, X_PASSES * P], U8, name="scales", align_bytes=64))
+            transpose_and_quantise(wx_raw[i], wx_codes[i], wx_scales[i], run)
+            if run == UNIT_RUNS - 1 and len(wx_raw) < BLOCKS:
                 wx_raw.append(load_unit(wx_rows(len(wx_raw))))
 
-        def multiply(i):
+        def multiply(i, run):
             gate, cell, quarter = block_order[i]
-            acc = sums.tile([P, P], F32, name="acc")
-            for g in range(X_PASSES):
+            if run == 0:
+                net_sums.append(sums.tile([P, P], F32, name="acc"))
+            acc = net_sums[i]
+            for g in range(run * RUN_PASSES, (run + 1) * RUN_PASSES):
                 cols = slice(g * P, (g + 1) * P)
                 nc.tensor.matmul_mx(
                     out=acc[:],
@@ -163,18 +175,18 @@ def tile_compute_gate_k_kernel(tc, input_word, hidden_states, Wx, bx, Wh, out_0,
                     start=(g == 0),
                     stop=False,
                 )
-            block = cell * 2 * BLOCKS_PER_GATE + gate * BLOCKS_PER_GATE + quarter
-            cols = slice(block * P, (block + 1) * P)
-            nc.tensor.matmul_mx(
-                out=acc[:],
-                lhsT=h_codes[:].bitcast(FP8X4),
-                lhsT_scale=h_scales[:],
-                rhs=wh_codes[:, cols].bitcast(FP8X4),
-                rhs_scale=wh_scales[:, cols],
-                start=False,
-                stop=True,
-            )
-            net_sums.append(acc)
+            if run == UNIT_RUNS - 1:
+                block = cell * 2 * BLOCKS_PER_GATE + gate * BLOCKS_PER_GATE + quarter
+                cols = slice(block * P, (block + 1) * P)
+                nc.tensor.matmul_mx(
+                    out=acc[:],
+                    lhsT=h_codes[:].bitcast(FP8X4),
+                    lhsT_scale=h_scales[:],
+                    rhs=wh_codes[:, cols].bitcast(FP8X4),
+                    rhs_scale=wh_scales[:, cols],
+                    start=False,
+                    stop=True,
+                )
 
         def finish(i):
             gate, cell, quarter = block_order[i]
@@ -195,10 +207,13 @@ def tile_compute_gate_k_kernel(tc, input_word, hidden_states, Wx, bx, Wh, out_0,
                 out = out_1 if gate == 0 else out_0
                 nc.sync.dma_start(out=out[:, cell, :], in_=result[:])
 
-        for i in range(BLOCKS + 2):
-            if i < BLOCKS:
-                prepare(i)
-            if 1 <= i <= BLOCKS:
-                multiply(i - 1)
-            if i >= 2:
-                finish(i - 2)
+        runs = BLOCKS * UNIT_RUNS
+        for r in range(runs + MULTIPLY_LAG + FINISH_LAG):
+            if r < runs:
+                prepare(r // UNIT_RUNS, r % UNIT_RUNS)
+            multiplied = r - MULTIPLY_LAG
+            if 0 <= multiplied < runs:
+                multiply(multiplied // UNIT_RUNS, multiplied % UNIT_RUNS)
+            closed = multiplied - FINISH_LAG
+            if closed >= 0 and closed % UNIT_RUNS == UNIT_RUNS - 1:
+                finish(closed // UNIT_RUNS)

@@ -18,52 +18,60 @@ K_PASS = P * PACK
 IN = 8192
 H = 512
 CELLS = 2
+GATES = 2
+OUT = CELLS * GATES * H
 X_PASSES = IN // K_PASS
-BLOCKS = CELLS * 2 * H // P
+BLOCKS = OUT // P
 BLOCKS_PER_GATE = H // P
 
 WORDS_PER_PASS = K_PASS // 2
 BANK_WORDS = 512
 PASSES_PER_BANK = BANK_WORDS // WORDS_PER_PASS
 UNIT_BANKS = X_PASSES // PASSES_PER_BANK
-RUN_BANKS = 4
-UNIT_RUNS = UNIT_BANKS // RUN_BANKS
-RUN_PASSES = RUN_BANKS * PASSES_PER_BANK
+LOAD_BANKS = 4
+LOAD_PASSES = LOAD_BANKS * PASSES_PER_BANK
+UNIT_LOADS = UNIT_BANKS // LOAD_BANKS
 
 QUANTISE_LAG = 2
 VECTOR_COPY_EVERY = 4
 
-MULTIPLY_LAG = 2
-FINISH_LAG = 1
-
-RAW_BUFS = 6
+RAW_UNITS = 6
 TRANSPOSE_BANKS = 6
 SUM_BANKS = 2
 
-FLOPS = 2 * P * (CELLS * 2 * H) * (IN + H)
+FLOPS = 2 * P * OUT * (IN + H)
 
 
 def tile_compute_gate_k_kernel(tc, input_word, hidden_states, Wx, bx, Wh, out_0, out_1):
     nc = tc.nc
     with ExitStack() as ctx:
         keep = ctx.enter_context(tc.tile_pool(name="keep", bufs=1))
-        raw_pool = ctx.enter_context(tc.tile_pool(name="raw", bufs=RAW_BUFS))
-        grouped_pool = ctx.enter_context(tc.tile_pool(name="grouped", bufs=QUANTISE_LAG + 3))
+        raw_pool = ctx.enter_context(tc.tile_pool(name="raw", bufs=RAW_UNITS * UNIT_LOADS))
+        grouped_pool = ctx.enter_context(tc.tile_pool(name="grouped", bufs=QUANTISE_LAG + 4))
         weight_pool = ctx.enter_context(tc.tile_pool(name="weight", bufs=3))
-        out_pool = ctx.enter_context(tc.tile_pool(name="out", bufs=2))
+        out_pool = ctx.enter_context(tc.tile_pool(name="out", bufs=3))
         banks = ctx.enter_context(tc.psum_pool(name="banks", bufs=TRANSPOSE_BANKS))
         sums = ctx.enter_context(tc.psum_pool(name="sums", bufs=SUM_BANKS))
         ctx.enter_context(tc.manual_schedule())
 
         def load_unit(rows):
-            raw = raw_pool.tile([P, IN], BF16, name="raw")
-            if rows.ndim == 2:
-                nc.sync.dma_start(out=raw[:], in_=rows)
-            else:
-                nc.sync.dma_start(out=raw[:].rearrange("p (b k) -> p b k", k=H), in_=rows)
-            return raw
+            parts = []
+            for part in range(UNIT_LOADS):
+                raw = raw_pool.tile([P, LOAD_PASSES * K_PASS], BF16, name="raw")
+                nc.sync.dma_start(
+                    out=raw[:].rearrange("p (g k) -> p g k", k=K_PASS),
+                    in_=rows[:, part * LOAD_PASSES : (part + 1) * LOAD_PASSES, :],
+                )
+                parts.append(raw)
+            return parts
 
-        def transpose_bank(words, passes, on_vector):
+        copied = []
+
+        def quantise(n):
+            grouped, codes, scales = copied[n]
+            nc.vector.quantize_mx(out=codes.bitcast(FP8X4), scales=scales, in_=grouped[:])
+
+        def transpose_bank(words, passes, codes, scales):
             bank = banks.tile([P, BANK_WORDS], F32, name="bank")
             for i in range(2 * passes):
                 cols = slice(i * P, (i + 1) * P)
@@ -71,51 +79,47 @@ def tile_compute_gate_k_kernel(tc, input_word, hidden_states, Wx, bx, Wh, out_0,
             grouped = grouped_pool.tile([P, passes * P * PACK], BF16, name="grouped", align_bytes=64)
             regrouped = bank[:, : 2 * passes * P].rearrange("p (g u r) -> p g r u", u=2, r=P)
             target = grouped[:].bitcast(F32).rearrange("p (g r u) -> p g r u", u=2, r=P)
-            if on_vector:
+            if len(copied) % VECTOR_COPY_EVERY == VECTOR_COPY_EVERY - 1:
                 nc.vector.tensor_copy(out=target, in_=regrouped)
             else:
                 nc.scalar.copy(out=target, in_=regrouped)
-            return grouped
+            copied.append((grouped, codes, scales))
+            if len(copied) > QUANTISE_LAG:
+                quantise(len(copied) - 1 - QUANTISE_LAG)
 
-        def transpose_and_quantise(raw, codes, scales, run):
-            words = raw[:].bitcast(F32)
-            grouped_tiles = []
-            for b in range(RUN_BANKS + QUANTISE_LAG):
-                if b < RUN_BANKS:
-                    first = (run * RUN_BANKS + b) * BANK_WORDS
-                    on_vector = b % VECTOR_COPY_EVERY == VECTOR_COPY_EVERY - 1
-                    grouped_tiles.append(
-                        transpose_bank(words[:, first : first + BANK_WORDS], PASSES_PER_BANK, on_vector)
-                    )
-                if b >= QUANTISE_LAG:
-                    ready = b - QUANTISE_LAG
-                    first = (run * RUN_BANKS + ready) * PASSES_PER_BANK * P
-                    cols = slice(first, first + PASSES_PER_BANK * P)
-                    nc.vector.quantize_mx(
-                        out=codes[:, cols].bitcast(FP8X4),
-                        scales=scales[:, cols],
-                        in_=grouped_tiles[ready][:],
-                    )
+        def transpose_unit(parts, codes, scales):
+            for b in range(UNIT_BANKS):
+                words = parts[b // LOAD_BANKS][:].bitcast(F32)
+                first = (b % LOAD_BANKS) * BANK_WORDS
+                cols = slice(b * PASSES_PER_BANK * P, (b + 1) * PASSES_PER_BANK * P)
+                transpose_bank(
+                    words[:, first : first + BANK_WORDS], PASSES_PER_BANK, codes[:, cols], scales[:, cols]
+                )
 
         block_order = []
-        for gate in range(2):
+        for gate in range(GATES):
             for cell in range(CELLS):
                 for quarter in range(BLOCKS_PER_GATE):
                     block_order.append((gate, cell, quarter))
 
-        def wx_rows(i):
+        def net_columns(i):
             gate, cell, quarter = block_order[i]
-            first = (gate * BLOCKS_PER_GATE + quarter) * P
-            return Wx[cell, first : first + P, :]
+            first = ((cell * GATES + gate) * BLOCKS_PER_GATE + quarter) * P
+            return slice(first, first + P)
 
-        x_raw = load_unit(input_word)
+        wx_blocks = Wx.rearrange("c n (g k) -> (c n) g k", k=K_PASS)
+        x_raw = load_unit(input_word.rearrange("b (g k) -> b g k", k=K_PASS))
         h_raw = keep.tile([P, H], BF16, name="h_raw")
         nc.sync.dma_start(out=h_raw[:], in_=hidden_states)
-        bias_rows = keep.tile([P, CELLS * 2 * H], BF16, name="bias_rows")
+        bias_rows = keep.tile([P, OUT], BF16, name="bias_rows")
         nc.vector.memset(bias_rows[:].bitcast(I32), 0)
         nc.sync.dma_start(out=bias_rows[0:1, :], in_=bx.rearrange("(o c) n -> o (c n)", o=1))
         wh_raw = load_unit(Wh.rearrange("c (b p) k -> p (c b) k", p=P))
-        wx_raw = [load_unit(wx_rows(i)) for i in range(RAW_BUFS - 2)]
+        wx_raw = [load_unit(wx_blocks[net_columns(i), :, :]) for i in range(RAW_UNITS - 2)]
+
+        def load_next_block():
+            if len(wx_raw) < BLOCKS:
+                wx_raw.append(load_unit(wx_blocks[net_columns(len(wx_raw)), :, :]))
 
         identity = keep.tile([P, P], F32, name="identity")
         masks.make_identity(nc, identity[:])
@@ -124,47 +128,43 @@ def tile_compute_gate_k_kernel(tc, input_word, hidden_states, Wx, bx, Wh, out_0,
 
         x_codes = keep.tile([P, X_PASSES * P], U32, name="x_codes", align_bytes=64)
         x_scales = keep.tile([P, X_PASSES * P], U8, name="x_scales", align_bytes=64)
-        for run in range(UNIT_RUNS):
-            transpose_and_quantise(x_raw, x_codes, x_scales, run)
-        wx_raw.append(load_unit(wx_rows(len(wx_raw))))
+        transpose_unit(x_raw, x_codes, x_scales)
+        load_next_block()
 
         h_codes = keep.tile([P, P], U32, name="h_codes", align_bytes=64)
         h_scales = keep.tile([P, P], U8, name="h_scales", align_bytes=64)
-        h_grouped = transpose_bank(h_raw[:].bitcast(F32), 1, False)
+        transpose_bank(h_raw[:].bitcast(F32), 1, h_codes[:], h_scales[:])
 
-        bias = keep.tile([P, CELLS * 2 * H], F32, name="bias")
-        for j in range(CELLS * 2 * H // BANK_WORDS):
+        bias = keep.tile([P, OUT], F32, name="bias")
+        for j in range(OUT // BANK_WORDS):
             cols = slice(j * BANK_WORDS, (j + 1) * BANK_WORDS)
             spread = banks.tile([P, BANK_WORDS], F32, name="bank")
             nc.tensor.matmul(out=spread[:], lhsT=ones[:], rhs=bias_rows[:, cols], start=True, stop=True)
             nc.vector.tensor_copy(out=bias[:, cols], in_=spread[:])
-        nc.vector.quantize_mx(out=h_codes[:].bitcast(FP8X4), scales=h_scales[:], in_=h_grouped[:])
 
         wh_codes = keep.tile([P, BLOCKS * P], U32, name="wh_codes", align_bytes=64)
         wh_scales = keep.tile([P, BLOCKS * P], U8, name="wh_scales", align_bytes=64)
-        for run in range(UNIT_RUNS):
-            transpose_and_quantise(wh_raw, wh_codes, wh_scales, run)
-        wx_raw.append(load_unit(wx_rows(len(wx_raw))))
+        transpose_unit(wh_raw, wh_codes, wh_scales)
+        load_next_block()
 
         wx_codes = []
         wx_scales = []
         net_sums = []
+        nets = []
         results = []
 
-        def prepare(i, run):
-            if run == 0:
-                wx_codes.append(weight_pool.tile([P, X_PASSES * P], U32, name="codes", align_bytes=64))
-                wx_scales.append(weight_pool.tile([P, X_PASSES * P], U8, name="scales", align_bytes=64))
-            transpose_and_quantise(wx_raw[i], wx_codes[i], wx_scales[i], run)
-            if run == UNIT_RUNS - 1 and len(wx_raw) < BLOCKS:
-                wx_raw.append(load_unit(wx_rows(len(wx_raw))))
+        def prepare(i):
+            wx_codes.append(weight_pool.tile([P, X_PASSES * P], U32, name="codes", align_bytes=64))
+            wx_scales.append(weight_pool.tile([P, X_PASSES * P], U8, name="scales", align_bytes=64))
+            transpose_unit(wx_raw[i], wx_codes[i], wx_scales[i])
+            load_next_block()
+            if i == BLOCKS - 1:
+                for n in range(len(copied) - QUANTISE_LAG, len(copied)):
+                    quantise(n)
 
-        def multiply(i, run):
-            gate, cell, quarter = block_order[i]
-            if run == 0:
-                net_sums.append(sums.tile([P, P], F32, name="acc"))
-            acc = net_sums[i]
-            for g in range(run * RUN_PASSES, (run + 1) * RUN_PASSES):
+        def multiply(i):
+            acc = sums.tile([P, P], F32, name="acc")
+            for g in range(X_PASSES):
                 cols = slice(g * P, (g + 1) * P)
                 nc.tensor.matmul_mx(
                     out=acc[:],
@@ -175,45 +175,42 @@ def tile_compute_gate_k_kernel(tc, input_word, hidden_states, Wx, bx, Wh, out_0,
                     start=(g == 0),
                     stop=False,
                 )
-            if run == UNIT_RUNS - 1:
-                block = cell * 2 * BLOCKS_PER_GATE + gate * BLOCKS_PER_GATE + quarter
-                cols = slice(block * P, (block + 1) * P)
-                nc.tensor.matmul_mx(
-                    out=acc[:],
-                    lhsT=h_codes[:].bitcast(FP8X4),
-                    lhsT_scale=h_scales[:],
-                    rhs=wh_codes[:, cols].bitcast(FP8X4),
-                    rhs_scale=wh_scales[:, cols],
-                    start=False,
-                    stop=True,
-                )
+            nc.tensor.matmul_mx(
+                out=acc[:],
+                lhsT=h_codes[:].bitcast(FP8X4),
+                lhsT_scale=h_scales[:],
+                rhs=wh_codes[:, net_columns(i)].bitcast(FP8X4),
+                rhs_scale=wh_scales[:, net_columns(i)],
+                start=False,
+                stop=True,
+            )
+            net_sums.append(acc)
 
-        def finish(i):
+        def add_bias(i):
+            net = out_pool.tile([P, P], F32, name="net")
+            nc.vector.tensor_tensor(out=net[:], in0=net_sums[i][:], in1=bias[:, net_columns(i)], op=ALU.add)
+            nets.append(net)
+
+        def activate(i):
             gate, cell, quarter = block_order[i]
-            block = cell * 2 * BLOCKS_PER_GATE + gate * BLOCKS_PER_GATE + quarter
             if quarter == 0:
                 results.append(out_pool.tile([P, H], F32, name="result"))
             result = results[-1]
-            net = out_pool.tile([P, P], F32, name="net")
-            nc.vector.tensor_tensor(
-                out=net[:], in0=net_sums[i][:], in1=bias[:, block * P : (block + 1) * P], op=ALU.add
-            )
             nc.scalar.activation(
                 out=result[:, quarter * P : (quarter + 1) * P],
-                in_=net[:],
+                in_=nets[i][:],
                 func=ACT.Sigmoid if gate == 0 else ACT.Tanh,
             )
             if quarter == BLOCKS_PER_GATE - 1:
                 out = out_1 if gate == 0 else out_0
                 nc.sync.dma_start(out=out[:, cell, :], in_=result[:])
 
-        runs = BLOCKS * UNIT_RUNS
-        for r in range(runs + MULTIPLY_LAG + FINISH_LAG):
-            if r < runs:
-                prepare(r // UNIT_RUNS, r % UNIT_RUNS)
-            multiplied = r - MULTIPLY_LAG
-            if 0 <= multiplied < runs:
-                multiply(multiplied // UNIT_RUNS, multiplied % UNIT_RUNS)
-            closed = multiplied - FINISH_LAG
-            if closed >= 0 and closed % UNIT_RUNS == UNIT_RUNS - 1:
-                finish(closed // UNIT_RUNS)
+        for i in range(BLOCKS + 3):
+            if i < BLOCKS:
+                prepare(i)
+            if 0 <= i - 1 < BLOCKS:
+                multiply(i - 1)
+            if 0 <= i - 2 < BLOCKS:
+                add_bias(i - 2)
+            if 0 <= i - 3 < BLOCKS:
+                activate(i - 3)

@@ -28,9 +28,9 @@ WORDS_PER_PASS = K_PASS // 2
 BANK_WORDS = 512
 PASSES_PER_BANK = BANK_WORDS // WORDS_PER_PASS
 UNIT_BANKS = X_PASSES // PASSES_PER_BANK
-LOAD_BANKS = 4
-LOAD_PASSES = LOAD_BANKS * PASSES_PER_BANK
-UNIT_LOADS = UNIT_BANKS // LOAD_BANKS
+UNIT_LOADS = 2
+LOAD_PASSES = X_PASSES // UNIT_LOADS
+X_LOADS = 4
 
 QUANTISE_LAG = 2
 VECTOR_COPY_EVERY = 4
@@ -87,10 +87,11 @@ def tile_compute_gate_k_kernel(tc, input_word, hidden_states, Wx, bx, Wh, out_0,
             if len(copied) > QUANTISE_LAG:
                 quantise(len(copied) - 1 - QUANTISE_LAG)
 
-        def transpose_unit(parts, codes, scales):
-            for b in range(UNIT_BANKS):
-                words = parts[b // LOAD_BANKS][:].bitcast(F32)
-                first = (b % LOAD_BANKS) * BANK_WORDS
+        def transpose_unit(parts, codes, scales, unit_banks):
+            part_banks = UNIT_BANKS // len(parts)
+            for b in unit_banks:
+                words = parts[b // part_banks][:].bitcast(F32)
+                first = (b % part_banks) * BANK_WORDS
                 cols = slice(b * PASSES_PER_BANK * P, (b + 1) * PASSES_PER_BANK * P)
                 transpose_bank(
                     words[:, first : first + BANK_WORDS], PASSES_PER_BANK, codes[:, cols], scales[:, cols]
@@ -108,14 +109,19 @@ def tile_compute_gate_k_kernel(tc, input_word, hidden_states, Wx, bx, Wh, out_0,
             return slice(first, first + P)
 
         wx_blocks = Wx.rearrange("c n (g k) -> (c n) g k", k=K_PASS)
-        x_raw = load_unit(input_word.rearrange("b (g k) -> b g k", k=K_PASS))
+        x_raw = []
+        for part in range(X_LOADS):
+            x_raw.append(keep.tile([P, IN // X_LOADS], BF16, name="x_raw%d" % part))
+            nc.sync.dma_start(
+                out=x_raw[part][:], in_=input_word[:, part * (IN // X_LOADS) : (part + 1) * (IN // X_LOADS)]
+            )
         h_raw = keep.tile([P, H], BF16, name="h_raw")
         nc.sync.dma_start(out=h_raw[:], in_=hidden_states)
         bias_rows = keep.tile([P, OUT], BF16, name="bias_rows")
         nc.vector.memset(bias_rows[:].bitcast(I32), 0)
         nc.sync.dma_start(out=bias_rows[0:1, :], in_=bx.rearrange("(o c) n -> o (c n)", o=1))
         wh_raw = load_unit(Wh.rearrange("c (b p) k -> p (c b) k", p=P))
-        wx_raw = [load_unit(wx_blocks[net_columns(i), :, :]) for i in range(RAW_UNITS - 2)]
+        wx_raw = [load_unit(wx_blocks[net_columns(i), :, :]) for i in range(RAW_UNITS - 1)]
 
         def load_next_block():
             if len(wx_raw) < BLOCKS:
@@ -125,11 +131,13 @@ def tile_compute_gate_k_kernel(tc, input_word, hidden_states, Wx, bx, Wh, out_0,
         masks.make_identity(nc, identity[:])
         ones = keep.tile([P, P], BF16, name="ones")
         nc.vector.memset(ones[:], 1.0)
+        early = keep.tile([P, 1], F32, name="early")
+        nc.vector.memset(early[:], 0.0)
+        nc.scalar.activation(out=early[:], in_=early[:], func=ACT.Sigmoid)
 
         x_codes = keep.tile([P, X_PASSES * P], U32, name="x_codes", align_bytes=64)
         x_scales = keep.tile([P, X_PASSES * P], U8, name="x_scales", align_bytes=64)
-        transpose_unit(x_raw, x_codes, x_scales)
-        load_next_block()
+        transpose_unit(x_raw, x_codes, x_scales, range(UNIT_BANKS))
 
         h_codes = keep.tile([P, P], U32, name="h_codes", align_bytes=64)
         h_scales = keep.tile([P, P], U8, name="h_scales", align_bytes=64)
@@ -144,7 +152,7 @@ def tile_compute_gate_k_kernel(tc, input_word, hidden_states, Wx, bx, Wh, out_0,
 
         wh_codes = keep.tile([P, BLOCKS * P], U32, name="wh_codes", align_bytes=64)
         wh_scales = keep.tile([P, BLOCKS * P], U8, name="wh_scales", align_bytes=64)
-        transpose_unit(wh_raw, wh_codes, wh_scales)
+        transpose_unit(wh_raw, wh_codes, wh_scales, range(UNIT_BANKS))
         load_next_block()
 
         wx_codes = []
@@ -153,10 +161,13 @@ def tile_compute_gate_k_kernel(tc, input_word, hidden_states, Wx, bx, Wh, out_0,
         nets = []
         results = []
 
-        def prepare(i):
+        def prepare_first_half(i):
             wx_codes.append(weight_pool.tile([P, X_PASSES * P], U32, name="codes", align_bytes=64))
             wx_scales.append(weight_pool.tile([P, X_PASSES * P], U8, name="scales", align_bytes=64))
-            transpose_unit(wx_raw[i], wx_codes[i], wx_scales[i])
+            transpose_unit(wx_raw[i], wx_codes[i], wx_scales[i], range(UNIT_BANKS // 2))
+
+        def prepare_second_half(i):
+            transpose_unit(wx_raw[i], wx_codes[i], wx_scales[i], range(UNIT_BANKS // 2, UNIT_BANKS))
             load_next_block()
             if i == BLOCKS - 1:
                 for n in range(len(copied) - QUANTISE_LAG, len(copied)):
@@ -207,10 +218,12 @@ def tile_compute_gate_k_kernel(tc, input_word, hidden_states, Wx, bx, Wh, out_0,
 
         for i in range(BLOCKS + 3):
             if i < BLOCKS:
-                prepare(i)
-            if 0 <= i - 1 < BLOCKS:
-                multiply(i - 1)
+                prepare_first_half(i)
             if 0 <= i - 2 < BLOCKS:
                 add_bias(i - 2)
             if 0 <= i - 3 < BLOCKS:
                 activate(i - 3)
+            if i < BLOCKS:
+                prepare_second_half(i)
+            if 0 <= i - 1 < BLOCKS:
+                multiply(i - 1)

@@ -159,7 +159,7 @@ def tile_compute_gate_k_kernel(tc, input_word, hidden_states, Wx, bx, Wh, out_0,
         wx_scales = []
         net_sums = []
         nets = []
-        results = []
+        results = keep.tile([P, GATES * CELLS, H], F32, name="results")
 
         def prepare_first_half(i):
             wx_codes.append(weight_pool.tile([P, X_PASSES * P], U32, name="codes", align_bytes=64))
@@ -173,21 +173,14 @@ def tile_compute_gate_k_kernel(tc, input_word, hidden_states, Wx, bx, Wh, out_0,
                 for n in range(len(copied) - QUANTISE_LAG, len(copied)):
                     quantise(n)
 
-        def multiply(i):
-            acc = sums.tile([P, P], F32, name="acc")
-            for g in range(X_PASSES):
-                cols = slice(g * P, (g + 1) * P)
-                nc.tensor.matmul_mx(
-                    out=acc[:],
-                    lhsT=x_codes[:, cols].bitcast(FP8X4),
-                    lhsT_scale=x_scales[:, cols],
-                    rhs=wx_codes[i][:, cols].bitcast(FP8X4),
-                    rhs_scale=wx_scales[i][:, cols],
-                    start=(g == 0),
-                    stop=False,
-                )
+        def multiply_first_half(i):
+            net_sums.append(sums.tile([P, P], F32, name="acc"))
+            multiply_input(i, range(X_PASSES // 2))
+
+        def multiply_second_half(i):
+            multiply_input(i, range(X_PASSES // 2, X_PASSES))
             nc.tensor.matmul_mx(
-                out=acc[:],
+                out=net_sums[i][:],
                 lhsT=h_codes[:].bitcast(FP8X4),
                 lhsT_scale=h_scales[:],
                 rhs=wh_codes[:, net_columns(i)].bitcast(FP8X4),
@@ -195,7 +188,19 @@ def tile_compute_gate_k_kernel(tc, input_word, hidden_states, Wx, bx, Wh, out_0,
                 start=False,
                 stop=True,
             )
-            net_sums.append(acc)
+
+        def multiply_input(i, passes):
+            for g in passes:
+                cols = slice(g * P, (g + 1) * P)
+                nc.tensor.matmul_mx(
+                    out=net_sums[i][:],
+                    lhsT=x_codes[:, cols].bitcast(FP8X4),
+                    lhsT_scale=x_scales[:, cols],
+                    rhs=wx_codes[i][:, cols].bitcast(FP8X4),
+                    rhs_scale=wx_scales[i][:, cols],
+                    start=(g == 0),
+                    stop=False,
+                )
 
         def add_bias(i):
             net = out_pool.tile([P, P], F32, name="net")
@@ -204,17 +209,11 @@ def tile_compute_gate_k_kernel(tc, input_word, hidden_states, Wx, bx, Wh, out_0,
 
         def activate(i):
             gate, cell, quarter = block_order[i]
-            if quarter == 0:
-                results.append(out_pool.tile([P, H], F32, name="result"))
-            result = results[-1]
             nc.scalar.activation(
-                out=result[:, quarter * P : (quarter + 1) * P],
+                out=results[:, i // BLOCKS_PER_GATE, quarter * P : (quarter + 1) * P],
                 in_=nets[i][:],
                 func=ACT.Sigmoid if gate == 0 else ACT.Tanh,
             )
-            if quarter == BLOCKS_PER_GATE - 1:
-                out = out_1 if gate == 0 else out_0
-                nc.sync.dma_start(out=out[:, cell, :], in_=result[:])
 
         for i in range(BLOCKS + 3):
             if i < BLOCKS:
@@ -223,7 +222,14 @@ def tile_compute_gate_k_kernel(tc, input_word, hidden_states, Wx, bx, Wh, out_0,
                 add_bias(i - 2)
             if 0 <= i - 3 < BLOCKS:
                 activate(i - 3)
+            if 0 <= i - 1 < BLOCKS:
+                multiply_first_half(i - 1)
             if i < BLOCKS:
                 prepare_second_half(i)
             if 0 <= i - 1 < BLOCKS:
-                multiply(i - 1)
+                multiply_second_half(i - 1)
+
+        for i in range(0, BLOCKS, BLOCKS_PER_GATE):
+            gate, cell, quarter = block_order[i]
+            out = out_1 if gate == 0 else out_0
+            nc.sync.dma_start(out=out[:, cell, :], in_=results[:, i // BLOCKS_PER_GATE, :])

from contextlib import ExitStack

import concourse.masks as masks
import concourse.mybir as mybir

F32 = mybir.dt.float32
BF16 = mybir.dt.bfloat16
I32 = mybir.dt.int32
U32 = mybir.dt.uint32
U8 = mybir.dt.uint8
FP8X4 = mybir.dt.float8_e4m3fn_x4
ACT = mybir.ActivationFunctionType
ALU = mybir.AluOpType

P = 128
PACK = 4
K_PASS = P * PACK
IN = 8192
H = 512
CELLS = 2
GATES = 2
OUT = CELLS * GATES * H
X_PASSES = IN // K_PASS
BLOCKS = OUT // P
BLOCKS_PER_GATE = H // P

WORDS_PER_PASS = K_PASS // 2
BANK_WORDS = 512
PASSES_PER_BANK = BANK_WORDS // WORDS_PER_PASS
UNIT_BANKS = X_PASSES // PASSES_PER_BANK
UNIT_LOADS = 2
LOAD_PASSES = X_PASSES // UNIT_LOADS
X_LOADS = 4

QUANTISE_LAG = 2
VECTOR_COPY_EVERY = 4

RAW_UNITS = 6
TRANSPOSE_BANKS = 6
SUM_BANKS = 2

FLOPS = 2 * P * OUT * (IN + H)


def tile_compute_gate_k_kernel(tc, input_word, hidden_states, Wx, bx, Wh, out_0, out_1):
    nc = tc.nc
    with ExitStack() as ctx:
        keep = ctx.enter_context(tc.tile_pool(name="keep", bufs=1))
        raw_pool = ctx.enter_context(tc.tile_pool(name="raw", bufs=RAW_UNITS * UNIT_LOADS))
        grouped_pool = ctx.enter_context(tc.tile_pool(name="grouped", bufs=QUANTISE_LAG + 4))
        weight_pool = ctx.enter_context(tc.tile_pool(name="weight", bufs=3))
        out_pool = ctx.enter_context(tc.tile_pool(name="out", bufs=3))
        banks = ctx.enter_context(tc.psum_pool(name="banks", bufs=TRANSPOSE_BANKS))
        sums = ctx.enter_context(tc.psum_pool(name="sums", bufs=SUM_BANKS))
        ctx.enter_context(tc.manual_schedule())

        def load_unit(rows):
            parts = []
            for part in range(UNIT_LOADS):
                raw = raw_pool.tile([P, LOAD_PASSES * K_PASS], BF16, name="raw")
                nc.sync.dma_start(
                    out=raw[:].rearrange("p (g k) -> p g k", k=K_PASS),
                    in_=rows[:, part * LOAD_PASSES : (part + 1) * LOAD_PASSES, :],
                )
                parts.append(raw)
            return parts

        copied = []

        def quantise(n):
            grouped, codes, scales = copied[n]
            nc.vector.quantize_mx(out=codes.bitcast(FP8X4), scales=scales, in_=grouped[:])

        def transpose_bank(words, passes, codes, scales):
            bank = banks.tile([P, BANK_WORDS], F32, name="bank")
            for i in range(2 * passes):
                cols = slice(i * P, (i + 1) * P)
                nc.tensor.transpose(bank[:, cols], words[:, cols], identity[:])
            grouped = grouped_pool.tile([P, passes * P * PACK], BF16, name="grouped", align_bytes=64)
            regrouped = bank[:, : 2 * passes * P].rearrange("p (g u r) -> p g r u", u=2, r=P)
            target = grouped[:].bitcast(F32).rearrange("p (g r u) -> p g r u", u=2, r=P)
            if len(copied) % VECTOR_COPY_EVERY == VECTOR_COPY_EVERY - 1:
                nc.vector.tensor_copy(out=target, in_=regrouped)
            else:
                nc.scalar.copy(out=target, in_=regrouped)
            copied.append((grouped, codes, scales))
            if len(copied) > QUANTISE_LAG:
                quantise(len(copied) - 1 - QUANTISE_LAG)

        def transpose_unit(parts, codes, scales, unit_banks):
            part_banks = UNIT_BANKS // len(parts)
            for b in unit_banks:
                words = parts[b // part_banks][:].bitcast(F32)
                first = (b % part_banks) * BANK_WORDS
                cols = slice(b * PASSES_PER_BANK * P, (b + 1) * PASSES_PER_BANK * P)
                transpose_bank(
                    words[:, first : first + BANK_WORDS], PASSES_PER_BANK, codes[:, cols], scales[:, cols]
                )

        block_order = []
        for gate in range(GATES):
            for cell in range(CELLS):
                for quarter in range(BLOCKS_PER_GATE):
                    block_order.append((gate, cell, quarter))

        def net_columns(i):
            gate, cell, quarter = block_order[i]
            first = ((cell * GATES + gate) * BLOCKS_PER_GATE + quarter) * P
            return slice(first, first + P)

        wx_blocks = Wx.rearrange("c n (g k) -> (c n) g k", k=K_PASS)
        x_raw = []
        for part in range(X_LOADS):
            x_raw.append(keep.tile([P, IN // X_LOADS], BF16, name="x_raw%d" % part))
            nc.sync.dma_start(
                out=x_raw[part][:], in_=input_word[:, part * (IN // X_LOADS) : (part + 1) * (IN // X_LOADS)]
            )
        h_raw = keep.tile([P, H], BF16, name="h_raw")
        nc.sync.dma_start(out=h_raw[:], in_=hidden_states)
        bias_rows = keep.tile([P, OUT], BF16, name="bias_rows")
        nc.vector.memset(bias_rows[:].bitcast(I32), 0)
        nc.sync.dma_start(out=bias_rows[0:1, :], in_=bx.rearrange("(o c) n -> o (c n)", o=1))
        wh_raw = load_unit(Wh.rearrange("c (b p) k -> p (c b) k", p=P))
        wx_raw = [load_unit(wx_blocks[net_columns(i), :, :]) for i in range(RAW_UNITS - 1)]

        def load_next_block():
            if len(wx_raw) < BLOCKS:
                wx_raw.append(load_unit(wx_blocks[net_columns(len(wx_raw)), :, :]))

        identity = keep.tile([P, P], F32, name="identity")
        masks.make_identity(nc, identity[:])
        ones = keep.tile([P, P], BF16, name="ones")
        nc.vector.memset(ones[:], 1.0)
        early = keep.tile([P, 1], F32, name="early")
        nc.vector.memset(early[:], 0.0)
        nc.scalar.activation(out=early[:], in_=early[:], func=ACT.Sigmoid)

        x_codes = keep.tile([P, X_PASSES * P], U32, name="x_codes", align_bytes=64)
        x_scales = keep.tile([P, X_PASSES * P], U8, name="x_scales", align_bytes=64)
        transpose_unit(x_raw, x_codes, x_scales, range(UNIT_BANKS))

        h_codes = keep.tile([P, P], U32, name="h_codes", align_bytes=64)
        h_scales = keep.tile([P, P], U8, name="h_scales", align_bytes=64)
        transpose_bank(h_raw[:].bitcast(F32), 1, h_codes[:], h_scales[:])

        bias = keep.tile([P, OUT], F32, name="bias")
        for j in range(OUT // BANK_WORDS):
            cols = slice(j * BANK_WORDS, (j + 1) * BANK_WORDS)
            spread = banks.tile([P, BANK_WORDS], F32, name="bank")
            nc.tensor.matmul(out=spread[:], lhsT=ones[:], rhs=bias_rows[:, cols], start=True, stop=True)
            nc.vector.tensor_copy(out=bias[:, cols], in_=spread[:])

        wh_codes = keep.tile([P, BLOCKS * P], U32, name="wh_codes", align_bytes=64)
        wh_scales = keep.tile([P, BLOCKS * P], U8, name="wh_scales", align_bytes=64)
        transpose_unit(wh_raw, wh_codes, wh_scales, range(UNIT_BANKS))
        load_next_block()

        wx_codes = []
        wx_scales = []
        net_sums = []
        nets = []
        results = keep.tile([P, GATES * CELLS, H], F32, name="results")

        def prepare_first_half(i):
            wx_codes.append(weight_pool.tile([P, X_PASSES * P], U32, name="codes", align_bytes=64))
            wx_scales.append(weight_pool.tile([P, X_PASSES * P], U8, name="scales", align_bytes=64))
            transpose_unit(wx_raw[i], wx_codes[i], wx_scales[i], range(UNIT_BANKS // 2))

        def prepare_second_half(i):
            transpose_unit(wx_raw[i], wx_codes[i], wx_scales[i], range(UNIT_BANKS // 2, UNIT_BANKS))
            load_next_block()
            if i == BLOCKS - 1:
                for n in range(len(copied) - QUANTISE_LAG, len(copied)):
                    quantise(n)

        def multiply_first_half(i):
            net_sums.append(sums.tile([P, P], F32, name="acc"))
            multiply_input(i, range(X_PASSES // 2))

        def multiply_second_half(i):
            multiply_input(i, range(X_PASSES // 2, X_PASSES))
            nc.tensor.matmul_mx(
                out=net_sums[i][:],
                lhsT=h_codes[:].bitcast(FP8X4),
                lhsT_scale=h_scales[:],
                rhs=wh_codes[:, net_columns(i)].bitcast(FP8X4),
                rhs_scale=wh_scales[:, net_columns(i)],
                start=False,
                stop=True,
            )

        def multiply_input(i, passes):
            for g in passes:
                cols = slice(g * P, (g + 1) * P)
                nc.tensor.matmul_mx(
                    out=net_sums[i][:],
                    lhsT=x_codes[:, cols].bitcast(FP8X4),
                    lhsT_scale=x_scales[:, cols],
                    rhs=wx_codes[i][:, cols].bitcast(FP8X4),
                    rhs_scale=wx_scales[i][:, cols],
                    start=(g == 0),
                    stop=False,
                )

        def add_bias(i):
            net = out_pool.tile([P, P], F32, name="net")
            nc.vector.tensor_tensor(out=net[:], in0=net_sums[i][:], in1=bias[:, net_columns(i)], op=ALU.add)
            nets.append(net)

        def activate(i):
            gate, cell, quarter = block_order[i]
            nc.scalar.activation(
                out=results[:, i // BLOCKS_PER_GATE, quarter * P : (quarter + 1) * P],
                in_=nets[i][:],
                func=ACT.Sigmoid if gate == 0 else ACT.Tanh,
            )

        for i in range(BLOCKS + 3):
            if i < BLOCKS:
                prepare_first_half(i)
            if 0 <= i - 2 < BLOCKS:
                add_bias(i - 2)
            if 0 <= i - 3 < BLOCKS:
                activate(i - 3)
            if 0 <= i - 1 < BLOCKS:
                multiply_first_half(i - 1)
            if i < BLOCKS:
                prepare_second_half(i)
            if 0 <= i - 1 < BLOCKS:
                multiply_second_half(i - 1)

        for i in range(0, BLOCKS, BLOCKS_PER_GATE):
            gate, cell, quarter = block_order[i]
            out = out_1 if gate == 0 else out_0
            nc.sync.dma_start(out=out[:, cell, :], in_=results[:, i // BLOCKS_PER_GATE, :])
